import numpy as np
import ml_dtypes


def mxq(x, axis, fmt="e4m3"):
    dtype, down = {"e4m3": (ml_dtypes.float8_e4m3fn, 7), "e5m2": (ml_dtypes.float8_e5m2, 14)}[fmt]
    v = np.moveaxis(np.asarray(x, np.float32).astype(ml_dtypes.bfloat16).astype(np.float64), axis, -1)
    blocks = v.reshape(v.shape[:-1] + (-1, 32))
    amax = np.abs(blocks).max(-1, keepdims=True)
    byte = np.maximum(np.where(amax > 0, np.frexp(amax)[1] - 1 + 127, 0) - down, 1)
    scale = np.exp2(byte - 127.0)
    codes = (blocks / scale).astype(np.float32).astype(dtype).astype(np.float64)
    return np.moveaxis((codes * scale).reshape(v.shape), -1, axis)


WIDE = False


def mx_kscale(k):
    if not WIDE:
        return np.ones(k)
    levels = np.array([10, -10, 5, -5, 0])
    if k % 512:
        return np.exp2(np.random.permutation(np.resize(levels, k // 32))).repeat(32)
    a = np.empty((k // 512, 16))
    for p in range(k // 512):
        a[p, :8] = np.random.permutation(np.resize(levels, 8))
        for g in range(8):
            far = levels[np.abs(levels - a[p, g]) >= 10]
            a[p, g + 8] = far[np.random.randint(len(far))]
    return np.exp2(a.ravel()).repeat(32)


BF16 = ml_dtypes.bfloat16


def bf(x):
    return np.asarray(x, np.float32).astype(BF16)


def f64(x):
    return np.asarray(x).astype(np.float64)


B, N, E, H, NOPE, VDIM, ROPE, QR, KVR = 2, 128, 512, 16, 32, 128, 32, 8192, 512
QH = NOPE + ROPE
BASE = 10000.0


def rope(v):
    d = v.shape[-1]
    n = v.shape[-2]
    theta = BASE ** (-2.0 * np.arange(d // 2) / d)
    ang = np.arange(n)[:, None] * theta[None, :]
    cos, sin = np.cos(ang), np.sin(ang)
    v1, v2 = v[..., 0::2], v[..., 1::2]
    return np.stack([v1 * cos - v2 * sin, v1 * sin + v2 * cos], axis=-1).reshape(v.shape)


def setup_inputs():
    s, t = mx_kscale(E), mx_kscale(QR)
    return {"x": bf(np.random.standard_normal((B, N, E)) * s),
            "Wqa": bf(np.random.standard_normal((E, QR)) / np.sqrt(E) / s[:, None] * t),
            "Wqb": bf(np.random.standard_normal((QR, H * QH)) / np.sqrt(QR) / t[:, None])}


def reference(x, Wqa, Wqb):
    cq = mxq(f64(x), 2, "e4m3") @ mxq(f64(Wqa), 0, "e4m3")
    q = mxq(cq, 2, "e4m3") @ mxq(f64(Wqb), 0, "e4m3")
    q = q.reshape(B, N, H, QH).transpose(0, 2, 1, 3)
    return np.concatenate([q[..., :NOPE], rope(q[..., NOPE:])], axis=-1)

@@ -1,0 +1,269 @@
+import math
+from contextlib import ExitStack
+
+import concourse.mybir as mybir
+from concourse.masks import make_identity
+
+F32 = mybir.dt.float32
+BF16 = mybir.dt.bfloat16
+U32 = mybir.dt.uint32
+U8 = mybir.dt.uint8
+FP8X4 = mybir.dt.float8_e4m3fn_x4
+ALU = mybir.AluOpType
+ACT = mybir.ActivationFunctionType
+
+B, N, E, H, NOPE, ROPE, QR = 2, 128, 512, 16, 32, 32, 8192
+QH = NOPE + ROPE
+HQ = H * QH
+BASE = 10000.0
+
+P = 128
+PACK = 4
+K_PASS = P * PACK
+BANK = 512
+
+N_GROUPS = QR // K_PASS
+HALVES = HQ // BANK
+HEADS_PER_HALF = BANK // QH
+PAIRS = ROPE // 2
+
+RUN = 4
+WQA_SCALAR_FOURS = 32
+RAW_BUFS = 8
+
+ROUND_MAGIC = 1.5 * 2.0**23
+
+FLOPS = 2 * B * N * E * QR + 2 * B * N * QR * HQ
+
+
+def tile_multilatentattention_pa_k_kernel(tc, x, Wqa, Wqb, out):
+    nc = tc.nc
+    with ExitStack() as ctx:
+        ctx.enter_context(tc.manual_schedule())
+        const = ctx.enter_context(tc.tile_pool(name="const", bufs=1))
+        raw = ctx.enter_context(tc.tile_pool(name="raw", bufs=RAW_BUFS))
+        work = ctx.enter_context(tc.tile_pool(name="work", bufs=3))
+        results = ctx.enter_context(tc.tile_pool(name="results", bufs=B * HALVES))
+        cq_psum = ctx.enter_context(tc.psum_pool(name="cq_psum", bufs=4))
+        q_psum = ctx.enter_context(tc.psum_pool(name="q_psum", bufs=1))
+
+        def regroup(copy, grouped, rows):
+            copy(
+                out=grouped.rearrange("p (c i) t -> p c t i", i=RUN),
+                in_=rows.rearrange("p t (c i) -> p c t i", i=RUN),
+            )
+
+        def quantise(words, scales, grouped):
+            nc.vector.quantize_mx(
+                out=words.bitcast(FP8X4),
+                scales=scales,
+                in_=grouped.rearrange("p w t -> p (w t)"),
+            )
+
+        x_rows = const.tile([P, B, E], BF16)
+        nc.sync.dma_start(out=x_rows[:], in_=x.rearrange("b n e -> n b e"))
+
+        position = const.tile([P, 1], F32)
+        nc.gpsimd.iota(
+            position[:],
+            pattern=[[0, 1]],
+            base=0,
+            channel_multiplier=1,
+            allow_small_or_imprecise_dtypes=True,
+        )
+        identity = const.tile([P, P], F32)
+        make_identity(nc, identity[:])
+
+        turns = const.tile([P, PAIRS], F32)
+        nc.gpsimd.tensor_scalar(
+            out=turns[:, 0:1], in0=position[:], scalar1=1.0 / (2.0 * math.pi), scalar2=None, op0=ALU.mult
+        )
+        ratio = BASE ** (-2.0 / ROPE)
+        filled = 1
+        while filled < PAIRS:
+            nc.gpsimd.tensor_scalar(
+                out=turns[:, filled : 2 * filled],
+                in0=turns[:, 0:filled],
+                scalar1=ratio**filled,
+                scalar2=None,
+                op0=ALU.mult,
+            )
+            filled *= 2
+        COS = slice(0, ROPE)
+        MINUS_SIN = slice(ROPE, ROPE + PAIRS)
+        PLUS_SIN = slice(ROPE + PAIRS, ROPE + 2 * PAIRS)
+        phase = const.tile([P, ROPE + 2 * PAIRS], F32)
+        nc.gpsimd.tensor_scalar(
+            out=phase[:, COS].rearrange("p (i e) -> p i e", e=2),
+            in0=turns[:].unsqueeze(2).to_broadcast([P, PAIRS, 2]),
+            scalar1=0.25,
+            scalar2=None,
+            op0=ALU.add,
+        )
+        nc.gpsimd.tensor_scalar(
+            out=phase[:, MINUS_SIN], in0=turns[:], scalar1=-1.0, scalar2=None, op0=ALU.mult
+        )
+        nc.gpsimd.tensor_copy(out=phase[:, PLUS_SIN], in_=turns[:])
+        whole = const.tile([P, ROPE + 2 * PAIRS], F32)
+        nc.gpsimd.tensor_scalar(
+            out=whole[:],
+            in0=phase[:],
+            scalar1=ROUND_MAGIC,
+            scalar2=ROUND_MAGIC,
+            op0=ALU.add,
+            op1=ALU.subtract,
+        )
+        part = const.tile([P, ROPE + 2 * PAIRS], F32)
+        nc.gpsimd.tensor_tensor(out=part[:], in0=phase[:], in1=whole[:], op=ALU.subtract)
+
+        x_pairs = x_rows[:].bitcast(F32).rearrange("n b (p u) -> n b u p", u=2)
+        x_turned = cq_psum.tile([P, PACK, P], F32, name="x_turned", tag="cq_bank")
+        for b in range(B):
+            for u in range(2):
+                nc.tensor.transpose(x_turned[:, 2 * b + u, :], x_pairs[:, b, u, :], identity[:])
+        x_grouped = const.tile([P, B * N, PACK], BF16, align_bytes=64)
+        nc.vector.tensor_copy(
+            out=x_grouped[:].bitcast(F32).rearrange("p (b n) u -> p b n u", b=B),
+            in_=x_turned[:].rearrange("p (b u) n -> p b n u", u=2),
+        )
+        x_words = const.tile([P, B * N], U32, align_bytes=64)
+        x_scales = const.tile([P, B * N], U8, align_bytes=64)
+        quantise(x_words[:], x_scales[:], x_grouped[:])
+
+        cq_words = const.tile([P, N_GROUPS, B * N], U32, align_bytes=64)
+        cq_scales = const.tile([P, N_GROUPS, B * N], U8, align_bytes=64)
+        q_sums = {}
+        for b in range(B):
+            for half in range(HALVES):
+                q_sums[(b, half)] = q_psum.tile(
+                    [P, BANK], F32, name="q_sums_%d_%d" % (b, half), tag="q_sums_%d_%d" % (b, half)
+                )
+        wqa_grouped, wqa_words, wqa_scales = {}, {}, {}
+        cq_banks, cq_grouped = {}, {}
+        wqb_grouped, wqb_words, wqb_scales = {}, {}, {}
+
+        def regroup_wqa(g):
+            rows = raw.tile([P, PACK, K_PASS], BF16, name="wqa_rows", tag="wqa_rows")
+            nc.sync.dma_start(
+                out=rows[:],
+                in_=Wqa[:, g * K_PASS : (g + 1) * K_PASS].rearrange("(p t) w -> p t w", t=PACK),
+            )
+            wqa_grouped[g] = work.tile(
+                [P, K_PASS, PACK], BF16, name="wqa_grouped", tag="wqa_grouped", align_bytes=64
+            )
+            placed = wqa_grouped[g][:].rearrange("p (t m) j -> p m j t", t=PACK)
+            columns = rows[:].rearrange("p j (m t) -> p m j t", t=PACK)
+            cut = WQA_SCALAR_FOURS
+            nc.scalar.copy(out=placed[:, 0:cut], in_=columns[:, 0:cut])
+            nc.vector.tensor_copy(out=placed[:, cut:P], in_=columns[:, cut:P])
+
+        def quantise_wqa(g):
+            wqa_words[g] = work.tile([P, K_PASS], U32, name="wqa_words", tag="wqa_words", align_bytes=64)
+            wqa_scales[g] = work.tile([P, K_PASS], U8, name="wqa_scales", tag="wqa_scales", align_bytes=64)
+            quantise(wqa_words[g][:], wqa_scales[g][:], wqa_grouped[g][:])
+
+        def first_product(g):
+            for b in range(B):
+                cq_banks[(g, b)] = cq_psum.tile([P, PACK, N], F32, name="cq_bank", tag="cq_bank")
+                for t in range(PACK):
+                    nc.tensor.matmul_mx(
+                        out=cq_banks[(g, b)][:, t, :],
+                        lhsT=wqa_words[g][:, t * P : (t + 1) * P].bitcast(FP8X4),
+                        lhsT_scale=wqa_scales[g][:, t * P : (t + 1) * P],
+                        rhs=x_words[:, b * N : (b + 1) * N].bitcast(FP8X4),
+                        rhs_scale=x_scales[:, b * N : (b + 1) * N],
+                        start=True,
+                        stop=True,
+                    )
+
+        def round_cq(g):
+            cq_grouped[g] = work.tile(
+                [P, B * N, PACK], BF16, name="cq_grouped", tag="cq_grouped", align_bytes=64
+            )
+            for b in range(B):
+                nc.scalar.copy(
+                    out=cq_grouped[g][:, b * N : (b + 1) * N, :],
+                    in_=cq_banks[(g, b)][:].rearrange("p t n -> p n t"),
+                )
+
+        def quantise_cq(g):
+            quantise(cq_words[:, g, :], cq_scales[:, g, :], cq_grouped[g][:])
+
+        def regroup_wqb(g):
+            rows = raw.tile([P, PACK, HQ], BF16, name="wqb_rows", tag="wqb_rows")
+            nc.sync.dma_start(
+                out=rows[:],
+                in_=Wqb[g * K_PASS : (g + 1) * K_PASS, :].rearrange("(p t) w -> p t w", t=PACK),
+            )
+            for half, copy in enumerate((nc.scalar.copy, nc.vector.tensor_copy)):
+                wqb_grouped[(g, half)] = work.tile(
+                    [P, BANK, PACK],
+                    BF16,
+                    name="wqb_grouped_%d" % half,
+                    tag="wqb_grouped_%d" % half,
+                    align_bytes=64,
+                )
+                regroup(copy, wqb_grouped[(g, half)][:], rows[:, :, half * BANK : (half + 1) * BANK])
+
+        def second_product(g):
+            for half in range(HALVES):
+                wqb_words[half] = work.tile(
+                    [P, BANK], U32, name="wqb_words_%d" % half, tag="wqb_words_%d" % half, align_bytes=64
+                )
+                wqb_scales[half] = work.tile(
+                    [P, BANK], U8, name="wqb_scales_%d" % half, tag="wqb_scales_%d" % half, align_bytes=64
+                )
+                quantise(wqb_words[half][:], wqb_scales[half][:], wqb_grouped[(g, half)][:])
+                for b in range(B):
+                    nc.tensor.matmul_mx(
+                        out=q_sums[(b, half)][:],
+                        lhsT=cq_words[:, g, b * N : (b + 1) * N].bitcast(FP8X4),
+                        lhsT_scale=cq_scales[:, g, b * N : (b + 1) * N],
+                        rhs=wqb_words[half][:].bitcast(FP8X4),
+                        rhs_scale=wqb_scales[half][:],
+                        start=(g == 0),
+                        stop=(g == N_GROUPS - 1),
+                    )
+
+        def run(stage, g):
+            if 0 <= g < N_GROUPS:
+                stage(g)
+
+        for step in range(2 * N_GROUPS + 1):
+            run(regroup_wqa, step)
+            run(regroup_wqb, step - N_GROUPS)
+            run(quantise_wqa, step - 1)
+            run(first_product, step - 1)
+            run(round_cq, step - 2)
+            run(quantise_cq, step - 3)
+            run(second_product, step - N_GROUPS - 1)
+
+        table = const.tile([P, ROPE + 2 * PAIRS], F32)
+        nc.scalar.activation(out=table[:], in_=part[:], func=ACT.Sin, scale=2.0 * math.pi)
+
+        def over_heads(part_of_table, width):
+            return table[:, part_of_table].unsqueeze(1).to_broadcast([P, HEADS_PER_HALF, width])
+
+        for half in range(HALVES):
+            for b in range(B):
+                q = q_sums[(b, half)][:].rearrange("p (h d) -> p h d", d=QH)
+                rotated = q[:, :, NOPE:QH]
+                pairs = rotated.rearrange("p h (i e) -> p h i e", e=2)
+                result = results.tile([P, HEADS_PER_HALF, QH], F32)
+                nc.scalar.copy(out=result[:, :, 0:NOPE], in_=q[:, :, 0:NOPE])
+                straight = results.tile([P, HEADS_PER_HALF, ROPE], F32)
+                nc.vector.tensor_mul(out=straight[:], in0=rotated, in1=over_heads(COS, ROPE))
+                crossed = results.tile([P, 2, HEADS_PER_HALF, PAIRS], F32)
+                nc.vector.tensor_mul(
+                    out=crossed[:, 0], in0=pairs[:, :, :, 1], in1=over_heads(MINUS_SIN, PAIRS)
+                )
+                nc.vector.tensor_mul(
+                    out=crossed[:, 1], in0=pairs[:, :, :, 0], in1=over_heads(PLUS_SIN, PAIRS)
+                )
+                nc.vector.tensor_add(
+                    out=result[:, :, NOPE:QH].rearrange("p h (i e) -> p h i e", e=2),
+                    in0=straight[:].rearrange("p h (i e) -> p h i e", e=2),
+                    in1=crossed[:].rearrange("p e h i -> p h i e"),
+                )
+                heads = slice(half * HEADS_PER_HALF, (half + 1) * HEADS_PER_HALF)
+                nc.sync.dma_start(out=out[b, heads].rearrange("h n d -> n h d"), in_=result[:])

@@ -29,6 +29,8 @@ PAIRS = ROPE // 2
 
 RUN = 4
 WQA_SCALAR_FOURS = 32
+WQB_TENSOR_COLUMNS = 256
+WQB_SCALAR_COLUMNS = 352
 RAW_BUFS = 8
 
 ROUND_MAGIC = 1.5 * 2.0**23
@@ -73,6 +75,8 @@ def tile_multilatentattention_pa_k_kernel(tc, x, Wqa, Wqb, out):
         )
         identity = const.tile([P, P], F32)
         make_identity(nc, identity[:])
+        identity_bf16 = const.tile([P, P], BF16)
+        make_identity(nc, identity_bf16[:])
 
         turns = const.tile([P, PAIRS], F32)
         nc.gpsimd.tensor_scalar(
@@ -140,6 +144,7 @@ def tile_multilatentattention_pa_k_kernel(tc, x, Wqa, Wqb, out):
                 )
         wqa_grouped, wqa_words, wqa_scales = {}, {}, {}
         cq_banks, cq_grouped = {}, {}
+        wqb_rows, wqb_turned = {}, {}
         wqb_grouped, wqb_words, wqb_scales = {}, {}, {}
 
         def regroup_wqa(g):
@@ -189,13 +194,26 @@ def tile_multilatentattention_pa_k_kernel(tc, x, Wqa, Wqb, out):
         def quantise_cq(g):
             quantise(cq_words[:, g, :], cq_scales[:, g, :], cq_grouped[g][:])
 
-        def regroup_wqb(g):
-            rows = raw.tile([P, PACK, HQ], BF16, name="wqb_rows", tag="wqb_rows")
+        def load_wqb(g):
+            wqb_rows[g] = raw.tile([P, PACK, HQ], BF16, name="wqb_rows", tag="wqb_rows")
             nc.sync.dma_start(
-                out=rows[:],
+                out=wqb_rows[g][:],
                 in_=Wqb[g * K_PASS : (g + 1) * K_PASS, :].rearrange("(p t) w -> p t w", t=PACK),
             )
-            for half, copy in enumerate((nc.scalar.copy, nc.vector.tensor_copy)):
+
+        def turn_wqb(g):
+            wqb_turned[g] = cq_psum.tile([P, WQB_TENSOR_COLUMNS, PACK], BF16, name="wqb_turned", tag="cq_bank")
+            for c in range(0, WQB_TENSOR_COLUMNS, P):
+                nc.tensor.matmul(
+                    out=wqb_turned[g][:, c : c + P, :],
+                    lhsT=identity_bf16[:],
+                    rhs=wqb_rows[g][:, :, c : c + P].rearrange("p t w -> p w t"),
+                    start=True,
+                    stop=True,
+                )
+
+        def regroup_wqb(g):
+            for half in range(HALVES):
                 wqb_grouped[(g, half)] = work.tile(
                     [P, BANK, PACK],
                     BF16,
@@ -203,7 +221,13 @@ def tile_multilatentattention_pa_k_kernel(tc, x, Wqa, Wqb, out):
                     tag="wqb_grouped_%d" % half,
                     align_bytes=64,
                 )
-                regroup(copy, wqb_grouped[(g, half)][:], rows[:, :, half * BANK : (half + 1) * BANK])
+            rows = wqb_rows[g]
+            first = WQB_TENSOR_COLUMNS
+            second = first + WQB_SCALAR_COLUMNS
+            nc.scalar.copy(out=wqb_grouped[(g, 0)][:, 0:first, :], in_=wqb_turned[g][:])
+            regroup(nc.scalar.copy, wqb_grouped[(g, 0)][:, first:BANK, :], rows[:, :, first:BANK])
+            regroup(nc.scalar.copy, wqb_grouped[(g, 1)][:, 0 : second - BANK, :], rows[:, :, BANK:second])
+            regroup(nc.vector.tensor_copy, wqb_grouped[(g, 1)][:, second - BANK : BANK, :], rows[:, :, second:HQ])
 
         def second_product(g):
             for half in range(HALVES):
@@ -231,6 +255,8 @@ def tile_multilatentattention_pa_k_kernel(tc, x, Wqa, Wqb, out):
 
         for step in range(2 * N_GROUPS + 1):
             run(regroup_wqa, step)
+            run(load_wqb, step - N_GROUPS + 1)
+            run(turn_wqb, step - N_GROUPS + 1)
             run(regroup_wqb, step - N_GROUPS)
             run(quantise_wqa, step - 1)
             run(first_product, step - 1)

@@ -205,9 +205,9 @@ def tile_multilatentattention_pa_k_kernel(tc, x, Wqa, Wqb, out):
             wqb_turned[g] = cq_psum.tile([P, WQB_TENSOR_COLUMNS, PACK], BF16, name="wqb_turned", tag="cq_bank")
             for c in range(0, WQB_TENSOR_COLUMNS, P):
                 nc.tensor.matmul(
-                    out=wqb_turned[g][:, c : c + P, :],
+                    out=wqb_turned[g][:, c : c + P, :].rearrange("p w t -> p t w"),
                     lhsT=identity_bf16[:],
-                    rhs=wqb_rows[g][:, :, c : c + P].rearrange("p t w -> p w t"),
+                    rhs=wqb_rows[g][:, :, c : c + P],
                     start=True,
                     stop=True,
                 )

@@ -28,9 +28,10 @@ HEADS_PER_HALF = BANK // QH
 PAIRS = ROPE // 2
 
 RUN = 4
-WQA_SCALAR_FOURS = 32
-WQB_TENSOR_COLUMNS = 256
-WQB_SCALAR_COLUMNS = 352
+WQA_TENSOR_FOURS = 32
+WQA_SCALAR_FOURS = 16
+WQB_TENSOR_COLUMNS = 128
+WQB_SCALAR_COLUMNS = 440
 RAW_BUFS = 8
 
 ROUND_MAGIC = 1.5 * 2.0**23
@@ -137,30 +138,46 @@ def tile_multilatentattention_pa_k_kernel(tc, x, Wqa, Wqb, out):
         cq_words = const.tile([P, N_GROUPS, B * N], U32, align_bytes=64)
         cq_scales = const.tile([P, N_GROUPS, B * N], U8, align_bytes=64)
         q_sums = {}
-        for b in range(B):
-            for half in range(HALVES):
-                q_sums[(b, half)] = q_psum.tile(
-                    [P, BANK], F32, name="q_sums_%d_%d" % (b, half), tag="q_sums_%d_%d" % (b, half)
-                )
+        wqa_rows, wqa_turned = {}, {}
         wqa_grouped, wqa_words, wqa_scales = {}, {}, {}
         cq_banks, cq_grouped = {}, {}
         wqb_rows, wqb_turned = {}, {}
         wqb_grouped, wqb_words, wqb_scales = {}, {}, {}
 
-        def regroup_wqa(g):
-            rows = raw.tile([P, PACK, K_PASS], BF16, name="wqa_rows", tag="wqa_rows")
+        def load_wqa(g):
+            wqa_rows[g] = raw.tile([P, PACK, K_PASS], BF16, name="wqa_rows", tag="wqa_rows")
             nc.sync.dma_start(
-                out=rows[:],
+                out=wqa_rows[g][:],
                 in_=Wqa[:, g * K_PASS : (g + 1) * K_PASS].rearrange("(p t) w -> p t w", t=PACK),
             )
+
+        def turn_wqa(g):
+            wqa_turned[g] = q_psum.tile(
+                [P, PACK, WQA_TENSOR_FOURS, PACK],
+                BF16,
+                name="wqa_turned_%d" % (g % 4),
+                tag="q_bank_%d" % (g % 4),
+            )
+            nc.tensor.matmul(
+                out=wqa_turned[g][:].rearrange("p t m j -> p j m t"),
+                lhsT=identity_bf16[:],
+                rhs=wqa_rows[g][:, :, 0 : PACK * WQA_TENSOR_FOURS].rearrange("p j (m t) -> p j m t", t=PACK),
+                start=True,
+                stop=True,
+            )
+
+        def regroup_wqa(g):
             wqa_grouped[g] = work.tile(
                 [P, K_PASS, PACK], BF16, name="wqa_grouped", tag="wqa_grouped", align_bytes=64
             )
+            by_place = wqa_grouped[g][:].rearrange("p (t m) j -> p t m j", t=PACK)
             placed = wqa_grouped[g][:].rearrange("p (t m) j -> p m j t", t=PACK)
-            columns = rows[:].rearrange("p j (m t) -> p m j t", t=PACK)
-            cut = WQA_SCALAR_FOURS
-            nc.scalar.copy(out=placed[:, 0:cut], in_=columns[:, 0:cut])
-            nc.vector.tensor_copy(out=placed[:, cut:P], in_=columns[:, cut:P])
+            columns = wqa_rows[g][:].rearrange("p j (m t) -> p m j t", t=PACK)
+            first = WQA_TENSOR_FOURS
+            second = first + WQA_SCALAR_FOURS
+            nc.scalar.copy(out=by_place[:, :, 0:first, :], in_=wqa_turned[g][:])
+            nc.scalar.copy(out=placed[:, first:second], in_=columns[:, first:second])
+            nc.vector.tensor_copy(out=placed[:, second:P], in_=columns[:, second:P])
 
         def quantise_wqa(g):
             wqa_words[g] = work.tile([P, K_PASS], U32, name="wqa_words", tag="wqa_words", align_bytes=64)
@@ -203,31 +220,23 @@ def tile_multilatentattention_pa_k_kernel(tc, x, Wqa, Wqb, out):
 
         def turn_wqb(g):
             wqb_turned[g] = cq_psum.tile([P, WQB_TENSOR_COLUMNS, PACK], BF16, name="wqb_turned", tag="cq_bank")
-            for c in range(0, WQB_TENSOR_COLUMNS, P):
-                nc.tensor.matmul(
-                    out=wqb_turned[g][:, c : c + P, :].rearrange("p w t -> p t w"),
-                    lhsT=identity_bf16[:],
-                    rhs=wqb_rows[g][:, :, c : c + P],
-                    start=True,
-                    stop=True,
-                )
+            nc.tensor.matmul(
+                out=wqb_turned[g][:].rearrange("p w t -> p t w"),
+                lhsT=identity_bf16[:],
+                rhs=wqb_rows[g][:, :, 0:WQB_TENSOR_COLUMNS],
+                start=True,
+                stop=True,
+            )
 
         def regroup_wqb(g):
-            for half in range(HALVES):
-                wqb_grouped[(g, half)] = work.tile(
-                    [P, BANK, PACK],
-                    BF16,
-                    name="wqb_grouped_%d" % half,
-                    tag="wqb_grouped_%d" % half,
-                    align_bytes=64,
-                )
-            rows = wqb_rows[g]
+            wqb_grouped[g] = work.tile(
+                [P, HQ, PACK], BF16, name="wqb_grouped", tag="wqb_grouped", align_bytes=64
+            )
             first = WQB_TENSOR_COLUMNS
             second = first + WQB_SCALAR_COLUMNS
-            nc.scalar.copy(out=wqb_grouped[(g, 0)][:, 0:first, :], in_=wqb_turned[g][:])
-            regroup(nc.scalar.copy, wqb_grouped[(g, 0)][:, first:BANK, :], rows[:, :, first:BANK])
-            regroup(nc.scalar.copy, wqb_grouped[(g, 1)][:, 0 : second - BANK, :], rows[:, :, BANK:second])
-            regroup(nc.vector.tensor_copy, wqb_grouped[(g, 1)][:, second - BANK : BANK, :], rows[:, :, second:HQ])
+            nc.scalar.copy(out=wqb_grouped[g][:, 0:first, :], in_=wqb_turned[g][:])
+            regroup(nc.scalar.copy, wqb_grouped[g][:, first:second, :], wqb_rows[g][:, :, first:second])
+            regroup(nc.vector.tensor_copy, wqb_grouped[g][:, second:HQ, :], wqb_rows[g][:, :, second:HQ])
 
         def second_product(g):
             for half in range(HALVES):
@@ -237,8 +246,17 @@ def tile_multilatentattention_pa_k_kernel(tc, x, Wqa, Wqb, out):
                 wqb_scales[half] = work.tile(
                     [P, BANK], U8, name="wqb_scales_%d" % half, tag="wqb_scales_%d" % half, align_bytes=64
                 )
-                quantise(wqb_words[half][:], wqb_scales[half][:], wqb_grouped[(g, half)][:])
+                quantise(
+                    wqb_words[half][:],
+                    wqb_scales[half][:],
+                    wqb_grouped[g][:, half * BANK : (half + 1) * BANK, :],
+                )
                 for b in range(B):
+                    if g == 0:
+                        bank = HALVES * b + half
+                        q_sums[(b, half)] = q_psum.tile(
+                            [P, BANK], F32, name="q_sums_%d" % bank, tag="q_bank_%d" % bank
+                        )
                     nc.tensor.matmul_mx(
                         out=q_sums[(b, half)][:],
                         lhsT=cq_words[:, g, b * N : (b + 1) * N].bitcast(FP8X4),
@@ -253,14 +271,18 @@ def tile_multilatentattention_pa_k_kernel(tc, x, Wqa, Wqb, out):
             if 0 <= g < N_GROUPS:
                 stage(g)
 
+        load_wqa(0)
+        turn_wqa(0)
         for step in range(2 * N_GROUPS + 1):
-            run(regroup_wqa, step)
+            run(load_wqa, step + 1)
             run(load_wqb, step - N_GROUPS + 1)
+            run(round_cq, step - 2)
+            run(regroup_wqa, step)
             run(turn_wqb, step - N_GROUPS + 1)
             run(regroup_wqb, step - N_GROUPS)
             run(quantise_wqa, step - 1)
             run(first_product, step - 1)
-            run(round_cq, step - 2)
+            run(turn_wqa, step + 1)
             run(quantise_cq, step - 3)
             run(second_product, step - N_GROUPS - 1)
 

@@ -29,9 +29,9 @@ PAIRS = ROPE // 2
 
 RUN = 4
 WQA_TENSOR_FOURS = 32
-WQA_SCALAR_FOURS = 16
+WQA_SCALAR_FOURS = 12
 WQB_TENSOR_COLUMNS = 128
-WQB_SCALAR_COLUMNS = 440
+WQB_SCALAR_COLUMNS = (144, 320, 416)
 RAW_BUFS = 8
 
 ROUND_MAGIC = 1.5 * 2.0**23
@@ -77,7 +77,7 @@ def tile_multilatentattention_pa_k_kernel(tc, x, Wqa, Wqb, out):
         identity = const.tile([P, P], F32)
         make_identity(nc, identity[:])
         identity_bf16 = const.tile([P, P], BF16)
-        make_identity(nc, identity_bf16[:])
+        nc.vector.tensor_copy(out=identity_bf16[:], in_=identity[:])
 
         turns = const.tile([P, PAIRS], F32)
         nc.gpsimd.tensor_scalar(
@@ -94,22 +94,19 @@ def tile_multilatentattention_pa_k_kernel(tc, x, Wqa, Wqb, out):
                 op0=ALU.mult,
             )
             filled *= 2
-        COS = slice(0, ROPE)
-        MINUS_SIN = slice(ROPE, ROPE + PAIRS)
-        PLUS_SIN = slice(ROPE + PAIRS, ROPE + 2 * PAIRS)
-        phase = const.tile([P, ROPE + 2 * PAIRS], F32)
+        phase = const.tile([P, 2, PAIRS, 2], F32)
         nc.gpsimd.tensor_scalar(
-            out=phase[:, COS].rearrange("p (i e) -> p i e", e=2),
+            out=phase[:, 0],
             in0=turns[:].unsqueeze(2).to_broadcast([P, PAIRS, 2]),
             scalar1=0.25,
             scalar2=None,
             op0=ALU.add,
         )
+        nc.gpsimd.tensor_copy(out=phase[:, 1, :, 0], in_=turns[:])
         nc.gpsimd.tensor_scalar(
-            out=phase[:, MINUS_SIN], in0=turns[:], scalar1=-1.0, scalar2=None, op0=ALU.mult
+            out=phase[:, 1, :, 1], in0=turns[:], scalar1=-1.0, scalar2=None, op0=ALU.mult
         )
-        nc.gpsimd.tensor_copy(out=phase[:, PLUS_SIN], in_=turns[:])
-        whole = const.tile([P, ROPE + 2 * PAIRS], F32)
+        whole = const.tile([P, 2, PAIRS, 2], F32)
         nc.gpsimd.tensor_scalar(
             out=whole[:],
             in0=phase[:],
@@ -118,7 +115,7 @@ def tile_multilatentattention_pa_k_kernel(tc, x, Wqa, Wqb, out):
             op0=ALU.add,
             op1=ALU.subtract,
         )
-        part = const.tile([P, ROPE + 2 * PAIRS], F32)
+        part = const.tile([P, 2, PAIRS, 2], F32)
         nc.gpsimd.tensor_tensor(out=part[:], in0=phase[:], in1=whole[:], op=ALU.subtract)
 
         x_pairs = x_rows[:].bitcast(F32).rearrange("n b (p u) -> n b u p", u=2)
@@ -127,13 +124,12 @@ def tile_multilatentattention_pa_k_kernel(tc, x, Wqa, Wqb, out):
             for u in range(2):
                 nc.tensor.transpose(x_turned[:, 2 * b + u, :], x_pairs[:, b, u, :], identity[:])
         x_grouped = const.tile([P, B * N, PACK], BF16, align_bytes=64)
-        nc.vector.tensor_copy(
+        nc.scalar.copy(
             out=x_grouped[:].bitcast(F32).rearrange("p (b n) u -> p b n u", b=B),
             in_=x_turned[:].rearrange("p (b u) n -> p b n u", u=2),
         )
         x_words = const.tile([P, B * N], U32, align_bytes=64)
         x_scales = const.tile([P, B * N], U8, align_bytes=64)
-        quantise(x_words[:], x_scales[:], x_grouped[:])
 
         cq_words = const.tile([P, N_GROUPS, B * N], U32, align_bytes=64)
         cq_scales = const.tile([P, N_GROUPS, B * N], U8, align_bytes=64)
@@ -142,7 +138,7 @@ def tile_multilatentattention_pa_k_kernel(tc, x, Wqa, Wqb, out):
         wqa_grouped, wqa_words, wqa_scales = {}, {}, {}
         cq_banks, cq_grouped = {}, {}
         wqb_rows, wqb_turned = {}, {}
-        wqb_grouped, wqb_words, wqb_scales = {}, {}, {}
+        wqb_grouped = {}
 
         def load_wqa(g):
             wqa_rows[g] = raw.tile([P, PACK, K_PASS], BF16, name="wqa_rows", tag="wqa_rows")
@@ -233,43 +229,44 @@ def tile_multilatentattention_pa_k_kernel(tc, x, Wqa, Wqb, out):
                 [P, HQ, PACK], BF16, name="wqb_grouped", tag="wqb_grouped", align_bytes=64
             )
             first = WQB_TENSOR_COLUMNS
-            second = first + WQB_SCALAR_COLUMNS
+            second = first + WQB_SCALAR_COLUMNS[min(g, 2)]
             nc.scalar.copy(out=wqb_grouped[g][:, 0:first, :], in_=wqb_turned[g][:])
             regroup(nc.scalar.copy, wqb_grouped[g][:, first:second, :], wqb_rows[g][:, :, first:second])
             regroup(nc.vector.tensor_copy, wqb_grouped[g][:, second:HQ, :], wqb_rows[g][:, :, second:HQ])
 
-        def second_product(g):
-            for half in range(HALVES):
-                wqb_words[half] = work.tile(
-                    [P, BANK], U32, name="wqb_words_%d" % half, tag="wqb_words_%d" % half, align_bytes=64
-                )
-                wqb_scales[half] = work.tile(
-                    [P, BANK], U8, name="wqb_scales_%d" % half, tag="wqb_scales_%d" % half, align_bytes=64
-                )
-                quantise(
-                    wqb_words[half][:],
-                    wqb_scales[half][:],
-                    wqb_grouped[g][:, half * BANK : (half + 1) * BANK, :],
-                )
-                for b in range(B):
-                    if g == 0:
-                        bank = HALVES * b + half
-                        q_sums[(b, half)] = q_psum.tile(
-                            [P, BANK], F32, name="q_sums_%d" % bank, tag="q_bank_%d" % bank
-                        )
-                    nc.tensor.matmul_mx(
-                        out=q_sums[(b, half)][:],
-                        lhsT=cq_words[:, g, b * N : (b + 1) * N].bitcast(FP8X4),
-                        lhsT_scale=cq_scales[:, g, b * N : (b + 1) * N],
-                        rhs=wqb_words[half][:].bitcast(FP8X4),
-                        rhs_scale=wqb_scales[half][:],
-                        start=(g == 0),
-                        stop=(g == N_GROUPS - 1),
+        def second_product(g, half):
+            words = work.tile(
+                [P, BANK], U32, name="wqb_words_%d" % half, tag="wqb_words_%d" % half, align_bytes=64
+            )
+            scales = work.tile(
+                [P, BANK], U8, name="wqb_scales_%d" % half, tag="wqb_scales_%d" % half, align_bytes=64
+            )
+            quantise(words[:], scales[:], wqb_grouped[g][:, half * BANK : (half + 1) * BANK, :])
+            for b in range(B):
+                if g == 0:
+                    bank = HALVES * b + half
+                    q_sums[(b, half)] = q_psum.tile(
+                        [P, BANK], F32, name="q_sums_%d" % bank, tag="q_bank_%d" % bank
                     )
+                nc.tensor.matmul_mx(
+                    out=q_sums[(b, half)][:],
+                    lhsT=cq_words[:, g, b * N : (b + 1) * N].bitcast(FP8X4),
+                    lhsT_scale=cq_scales[:, g, b * N : (b + 1) * N],
+                    rhs=words[:].bitcast(FP8X4),
+                    rhs_scale=scales[:],
+                    start=(g == 0),
+                    stop=(g == N_GROUPS - 1),
+                )
+
+        table = const.tile([P, 2, PAIRS, 2], F32)
 
         def run(stage, g):
             if 0 <= g < N_GROUPS:
                 stage(g)
+
+        products = {g + 1: [(g, half) for half in range(HALVES)] for g in range(N_GROUPS)}
+        products[N_GROUPS - 1] = [(N_GROUPS - 2, 0)]
+        products[N_GROUPS] = [(N_GROUPS - 1, 0), (N_GROUPS - 2, 1), (N_GROUPS - 1, 1)]
 
         load_wqa(0)
         turn_wqa(0)
@@ -278,40 +275,54 @@ def tile_multilatentattention_pa_k_kernel(tc, x, Wqa, Wqb, out):
             run(load_wqb, step - N_GROUPS + 1)
             run(round_cq, step - 2)
             run(regroup_wqa, step)
+            if step == 0:
+                quantise(x_words[:], x_scales[:], x_grouped[:])
+            if step == 1:
+                nc.scalar.activation(out=table[:], in_=part[:], func=ACT.Sin, scale=2.0 * math.pi)
             run(turn_wqb, step - N_GROUPS + 1)
             run(regroup_wqb, step - N_GROUPS)
             run(quantise_wqa, step - 1)
             run(first_product, step - 1)
             run(turn_wqa, step + 1)
             run(quantise_cq, step - 3)
-            run(second_product, step - N_GROUPS - 1)
+            for g, half in products.get(step - N_GROUPS, []):
+                second_product(g, half)
 
-        table = const.tile([P, ROPE + 2 * PAIRS], F32)
-        nc.scalar.activation(out=table[:], in_=part[:], func=ACT.Sin, scale=2.0 * math.pi)
+        def store(b, half, h0, h1, result):
+            heads = slice(half * HEADS_PER_HALF + h0, half * HEADS_PER_HALF + h1)
+            nc.sync.dma_start(out=out[b, heads].rearrange("h n d -> n h d"), in_=result[:, h0:h1])
 
-        def over_heads(part_of_table, width):
-            return table[:, part_of_table].unsqueeze(1).to_broadcast([P, HEADS_PER_HALF, width])
+        def multiply(q, terms, h0, h1):
+            wide = [P, 2, h1 - h0, ROPE]
+            nc.vector.tensor_mul(
+                out=terms[:, :, h0:h1],
+                in0=q[:, h0:h1, NOPE:QH].unsqueeze(1).to_broadcast(wide),
+                in1=table[:].rearrange("p r i e -> p r (i e)").unsqueeze(2).to_broadcast(wide),
+            )
+
+        def add(engine, result, terms, h0, h1):
+            engine.tensor_tensor(
+                out=result[:, h0:h1, NOPE:QH].rearrange("p h (i e) -> p h i e", e=2),
+                in0=terms[:, 0, h0:h1].rearrange("p h (i e) -> p h i e", e=2),
+                in1=terms[:, 1, h0:h1].rearrange("p h (i e) -> p h i e", e=2)[:, :, :, ::-1],
+                op=ALU.add,
+            )
 
         for half in range(HALVES):
             for b in range(B):
                 q = q_sums[(b, half)][:].rearrange("p (h d) -> p h d", d=QH)
-                rotated = q[:, :, NOPE:QH]
-                pairs = rotated.rearrange("p h (i e) -> p h i e", e=2)
                 result = results.tile([P, HEADS_PER_HALF, QH], F32)
+                terms = results.tile([P, 2, HEADS_PER_HALF, ROPE], F32)
                 nc.scalar.copy(out=result[:, :, 0:NOPE], in_=q[:, :, 0:NOPE])
-                straight = results.tile([P, HEADS_PER_HALF, ROPE], F32)
-                nc.vector.tensor_mul(out=straight[:], in0=rotated, in1=over_heads(COS, ROPE))
-                crossed = results.tile([P, 2, HEADS_PER_HALF, PAIRS], F32)
-                nc.vector.tensor_mul(
-                    out=crossed[:, 0], in0=pairs[:, :, :, 1], in1=over_heads(MINUS_SIN, PAIRS)
-                )
-                nc.vector.tensor_mul(
-                    out=crossed[:, 1], in0=pairs[:, :, :, 0], in1=over_heads(PLUS_SIN, PAIRS)
-                )
-                nc.vector.tensor_add(
-                    out=result[:, :, NOPE:QH].rearrange("p h (i e) -> p h i e", e=2),
-                    in0=straight[:].rearrange("p h (i e) -> p h i e", e=2),
-                    in1=crossed[:].rearrange("p e h i -> p h i e"),
-                )
-                heads = slice(half * HEADS_PER_HALF, (half + 1) * HEADS_PER_HALF)
-                nc.sync.dma_start(out=out[b, heads].rearrange("h n d -> n h d"), in_=result[:])
+                if (half, b) != (HALVES - 1, B - 1):
+                    multiply(q, terms, 0, HEADS_PER_HALF)
+                    add(nc.gpsimd, result, terms, 0, HEADS_PER_HALF)
+                    store(b, half, 0, HEADS_PER_HALF, result)
+                else:
+                    middle = HEADS_PER_HALF // 2
+                    parts = ((0, middle), (middle, HEADS_PER_HALF))
+                    for h0, h1 in parts:
+                        multiply(q, terms, h0, h1)
+                    for h0, h1 in parts:
+                        add(nc.vector, result, terms, h0, h1)
+                        store(b, half, h0, h1, result)

@@ -29,9 +29,9 @@ PAIRS = ROPE // 2
 
 RUN = 4
 WQA_TENSOR_FOURS = 32
-WQA_SCALAR_FOURS = 12
+WQA_SCALAR_FOURS = 16
 WQB_TENSOR_COLUMNS = 128
-WQB_SCALAR_COLUMNS = (144, 320, 416)
+WQB_SCALAR_COLUMNS = (144, 320, 440)
 RAW_BUFS = 8
 
 ROUND_MAGIC = 1.5 * 2.0**23
@@ -76,17 +76,20 @@ def tile_multilatentattention_pa_k_kernel(tc, x, Wqa, Wqb, out):
         )
         identity = const.tile([P, P], F32)
         make_identity(nc, identity[:])
-        identity_bf16 = const.tile([P, P], BF16)
-        nc.vector.tensor_copy(out=identity_bf16[:], in_=identity[:])
 
         turns = const.tile([P, PAIRS], F32)
-        nc.gpsimd.tensor_scalar(
-            out=turns[:, 0:1], in0=position[:], scalar1=1.0 / (2.0 * math.pi), scalar2=None, op0=ALU.mult
-        )
         ratio = BASE ** (-2.0 / ROPE)
-        filled = 1
+        filled = 4
+        for i in range(filled):
+            nc.vector.tensor_scalar(
+                out=turns[:, i : i + 1],
+                in0=position[:],
+                scalar1=ratio**i / (2.0 * math.pi),
+                scalar2=None,
+                op0=ALU.mult,
+            )
         while filled < PAIRS:
-            nc.gpsimd.tensor_scalar(
+            nc.vector.tensor_scalar(
                 out=turns[:, filled : 2 * filled],
                 in0=turns[:, 0:filled],
                 scalar1=ratio**filled,
@@ -95,19 +98,19 @@ def tile_multilatentattention_pa_k_kernel(tc, x, Wqa, Wqb, out):
             )
             filled *= 2
         phase = const.tile([P, 2, PAIRS, 2], F32)
-        nc.gpsimd.tensor_scalar(
+        nc.vector.tensor_scalar(
             out=phase[:, 0],
             in0=turns[:].unsqueeze(2).to_broadcast([P, PAIRS, 2]),
             scalar1=0.25,
             scalar2=None,
             op0=ALU.add,
         )
-        nc.gpsimd.tensor_copy(out=phase[:, 1, :, 0], in_=turns[:])
-        nc.gpsimd.tensor_scalar(
+        nc.vector.tensor_copy(out=phase[:, 1, :, 0], in_=turns[:])
+        nc.vector.tensor_scalar(
             out=phase[:, 1, :, 1], in0=turns[:], scalar1=-1.0, scalar2=None, op0=ALU.mult
         )
         whole = const.tile([P, 2, PAIRS, 2], F32)
-        nc.gpsimd.tensor_scalar(
+        nc.vector.tensor_scalar(
             out=whole[:],
             in0=phase[:],
             scalar1=ROUND_MAGIC,
@@ -116,7 +119,10 @@ def tile_multilatentattention_pa_k_kernel(tc, x, Wqa, Wqb, out):
             op1=ALU.subtract,
         )
         part = const.tile([P, 2, PAIRS, 2], F32)
-        nc.gpsimd.tensor_tensor(out=part[:], in0=phase[:], in1=whole[:], op=ALU.subtract)
+        nc.vector.tensor_tensor(out=part[:], in0=phase[:], in1=whole[:], op=ALU.subtract)
+
+        identity_bf16 = const.tile([P, P], BF16)
+        nc.vector.tensor_copy(out=identity_bf16[:], in_=identity[:])
 
         x_pairs = x_rows[:].bitcast(F32).rearrange("n b (p u) -> n b u p", u=2)
         x_turned = cq_psum.tile([P, PACK, P], F32, name="x_turned", tag="cq_bank")

@@ -29,9 +29,9 @@ PAIRS = ROPE // 2
 
 RUN = 4
 WQA_TENSOR_FOURS = 32
-WQA_SCALAR_FOURS = 16
+WQA_SCALAR_FOURS = (0, 0, 0, 12)
 WQB_TENSOR_COLUMNS = 128
-WQB_SCALAR_COLUMNS = (144, 320, 440)
+WQB_SCALAR_COLUMNS = (144, 320, 416)
 RAW_BUFS = 8
 
 ROUND_MAGIC = 1.5 * 2.0**23
@@ -176,9 +176,10 @@ def tile_multilatentattention_pa_k_kernel(tc, x, Wqa, Wqb, out):
             placed = wqa_grouped[g][:].rearrange("p (t m) j -> p m j t", t=PACK)
             columns = wqa_rows[g][:].rearrange("p j (m t) -> p m j t", t=PACK)
             first = WQA_TENSOR_FOURS
-            second = first + WQA_SCALAR_FOURS
+            second = first + WQA_SCALAR_FOURS[min(g, len(WQA_SCALAR_FOURS) - 1)]
             nc.scalar.copy(out=by_place[:, :, 0:first, :], in_=wqa_turned[g][:])
-            nc.scalar.copy(out=placed[:, first:second], in_=columns[:, first:second])
+            if second > first:
+                nc.scalar.copy(out=placed[:, first:second], in_=columns[:, first:second])
             nc.vector.tensor_copy(out=placed[:, second:P], in_=columns[:, second:P])
 
         def quantise_wqa(g):
@@ -235,12 +236,16 @@ def tile_multilatentattention_pa_k_kernel(tc, x, Wqa, Wqb, out):
                 [P, HQ, PACK], BF16, name="wqb_grouped", tag="wqb_grouped", align_bytes=64
             )
             first = WQB_TENSOR_COLUMNS
-            second = first + WQB_SCALAR_COLUMNS[min(g, 2)]
+            second = first + WQB_SCALAR_COLUMNS[min(g, len(WQB_SCALAR_COLUMNS) - 1)]
             nc.scalar.copy(out=wqb_grouped[g][:, 0:first, :], in_=wqb_turned[g][:])
             regroup(nc.scalar.copy, wqb_grouped[g][:, first:second, :], wqb_rows[g][:, :, first:second])
             regroup(nc.vector.tensor_copy, wqb_grouped[g][:, second:HQ, :], wqb_rows[g][:, :, second:HQ])
 
-        def second_product(g, half):
+        def second_product(g):
+            for half in range(HALVES):
+                multiply_half(g, half)
+
+        def multiply_half(g, half):
             words = work.tile(
                 [P, BANK], U32, name="wqb_words_%d" % half, tag="wqb_words_%d" % half, align_bytes=64
             )
@@ -270,10 +275,6 @@ def tile_multilatentattention_pa_k_kernel(tc, x, Wqa, Wqb, out):
             if 0 <= g < N_GROUPS:
                 stage(g)
 
-        products = {g + 1: [(g, half) for half in range(HALVES)] for g in range(N_GROUPS)}
-        products[N_GROUPS - 1] = [(N_GROUPS - 2, 0)]
-        products[N_GROUPS] = [(N_GROUPS - 1, 0), (N_GROUPS - 2, 1), (N_GROUPS - 1, 1)]
-
         load_wqa(0)
         turn_wqa(0)
         for step in range(2 * N_GROUPS + 1):
@@ -291,8 +292,7 @@ def tile_multilatentattention_pa_k_kernel(tc, x, Wqa, Wqb, out):
             run(first_product, step - 1)
             run(turn_wqa, step + 1)
             run(quantise_cq, step - 3)
-            for g, half in products.get(step - N_GROUPS, []):
-                second_product(g, half)
+            run(second_product, step - N_GROUPS - 1)
 
         def store(b, half, h0, h1, result):
             heads = slice(half * HEADS_PER_HALF + h0, half * HEADS_PER_HALF + h1)
@@ -314,21 +314,23 @@ def tile_multilatentattention_pa_k_kernel(tc, x, Wqa, Wqb, out):
                 op=ALU.add,
             )
 
+        middle = HEADS_PER_HALF // 2
+        parts = ((0, middle), (middle, HEADS_PER_HALF))
+        pieces = []
         for half in range(HALVES):
             for b in range(B):
                 q = q_sums[(b, half)][:].rearrange("p (h d) -> p h d", d=QH)
                 result = results.tile([P, HEADS_PER_HALF, QH], F32)
                 terms = results.tile([P, 2, HEADS_PER_HALF, ROPE], F32)
                 nc.scalar.copy(out=result[:, :, 0:NOPE], in_=q[:, :, 0:NOPE])
-                if (half, b) != (HALVES - 1, B - 1):
-                    multiply(q, terms, 0, HEADS_PER_HALF)
-                    add(nc.gpsimd, result, terms, 0, HEADS_PER_HALF)
-                    store(b, half, 0, HEADS_PER_HALF, result)
-                else:
-                    middle = HEADS_PER_HALF // 2
-                    parts = ((0, middle), (middle, HEADS_PER_HALF))
-                    for h0, h1 in parts:
-                        multiply(q, terms, h0, h1)
-                    for h0, h1 in parts:
-                        add(nc.vector, result, terms, h0, h1)
+                last = (half, b) == (HALVES - 1, B - 1)
+                for h0, h1 in parts if last else ((0, HEADS_PER_HALF),):
+                    multiply(q, terms, h0, h1)
+                    if half == 0:
+                        add(nc.gpsimd, result, terms, h0, h1)
                         store(b, half, h0, h1, result)
+                    else:
+                        pieces.append((b, half, h0, h1, result, terms))
+        for b, half, h0, h1, result, terms in pieces:
+            add(nc.vector, result, terms, h0, h1)
+            store(b, half, h0, h1, result)

@@ -27,7 +27,7 @@ HALVES = HQ // BANK
 HEADS_PER_HALF = BANK // QH
 PAIRS = ROPE // 2
 
-RUN = 4
+RUN = 8
 WQA_TENSOR_FOURS = 32
 WQA_SCALAR_FOURS = (0, 0, 0, 12)
 WQB_TENSOR_COLUMNS = 128

@@ -202,17 +202,23 @@ def tile_multilatentattention_pa_k_kernel(tc, x, Wqa, Wqb, out):
                     )
 
         def round_cq(g):
-            cq_grouped[g] = work.tile(
-                [P, B * N, PACK], BF16, name="cq_grouped", tag="cq_grouped", align_bytes=64
-            )
+            if g % 2 == 0:
+                cq_grouped[g // 2] = work.tile(
+                    [P, 2, B * N, PACK], BF16, name="cq_grouped", tag="cq_grouped", align_bytes=64
+                )
             for b in range(B):
                 nc.scalar.copy(
-                    out=cq_grouped[g][:, b * N : (b + 1) * N, :],
+                    out=cq_grouped[g // 2][:, g % 2, b * N : (b + 1) * N, :],
                     in_=cq_banks[(g, b)][:].rearrange("p t n -> p n t"),
                 )
 
         def quantise_cq(g):
-            quantise(cq_words[:, g, :], cq_scales[:, g, :], cq_grouped[g][:])
+            if g % 2 == 1:
+                quantise(
+                    cq_words[:, g - 1 : g + 1, :].rearrange("p g n -> p (g n)"),
+                    cq_scales[:, g - 1 : g + 1, :].rearrange("p g n -> p (g n)"),
+                    cq_grouped[g // 2][:].rearrange("p g n t -> p (g n) t"),
+                )
 
         def load_wqb(g):
             wqb_rows[g] = raw.tile([P, PACK, HQ], BF16, name="wqb_rows", tag="wqb_rows")
@@ -222,7 +228,11 @@ def tile_multilatentattention_pa_k_kernel(tc, x, Wqa, Wqb, out):
             )
 
         def turn_wqb(g):
-            wqb_turned[g] = cq_psum.tile([P, WQB_TENSOR_COLUMNS, PACK], BF16, name="wqb_turned", tag="cq_bank")
+            shape = [P, WQB_TENSOR_COLUMNS, PACK]
+            if g < 2:
+                wqb_turned[g] = q_psum.tile(shape, BF16, name="wqb_turned_%d" % g, tag="q_bank_%d" % g)
+            else:
+                wqb_turned[g] = cq_psum.tile(shape, BF16, name="wqb_turned", tag="cq_bank")
             nc.tensor.matmul(
                 out=wqb_turned[g][:].rearrange("p w t -> p t w"),
                 lhsT=identity_bf16[:],
@@ -242,32 +252,29 @@ def tile_multilatentattention_pa_k_kernel(tc, x, Wqa, Wqb, out):
             regroup(nc.vector.tensor_copy, wqb_grouped[g][:, second:HQ, :], wqb_rows[g][:, :, second:HQ])
 
         def second_product(g):
+            words = work.tile([P, HQ], U32, name="wqb_words", tag="wqb_words", align_bytes=64)
+            scales = work.tile([P, HQ], U8, name="wqb_scales", tag="wqb_scales", align_bytes=64)
+            width = HQ if g < N_GROUPS - 1 else BANK
+            for c in range(0, HQ, width):
+                cols = slice(c, c + width)
+                quantise(words[:, cols], scales[:, cols], wqb_grouped[g][:, cols, :])
             for half in range(HALVES):
-                multiply_half(g, half)
-
-        def multiply_half(g, half):
-            words = work.tile(
-                [P, BANK], U32, name="wqb_words_%d" % half, tag="wqb_words_%d" % half, align_bytes=64
-            )
-            scales = work.tile(
-                [P, BANK], U8, name="wqb_scales_%d" % half, tag="wqb_scales_%d" % half, align_bytes=64
-            )
-            quantise(words[:], scales[:], wqb_grouped[g][:, half * BANK : (half + 1) * BANK, :])
-            for b in range(B):
-                if g == 0:
-                    bank = HALVES * b + half
-                    q_sums[(b, half)] = q_psum.tile(
-                        [P, BANK], F32, name="q_sums_%d" % bank, tag="q_bank_%d" % bank
+                cols = slice(half * BANK, (half + 1) * BANK)
+                for b in range(B):
+                    if g == 0:
+                        bank = HALVES * b + half
+                        q_sums[(b, half)] = q_psum.tile(
+                            [P, BANK], F32, name="q_sums_%d" % bank, tag="q_bank_%d" % bank
+                        )
+                    nc.tensor.matmul_mx(
+                        out=q_sums[(b, half)][:],
+                        lhsT=cq_words[:, g, b * N : (b + 1) * N].bitcast(FP8X4),
+                        lhsT_scale=cq_scales[:, g, b * N : (b + 1) * N],
+                        rhs=words[:, cols].bitcast(FP8X4),
+                        rhs_scale=scales[:, cols],
+                        start=(g == 0),
+                        stop=(g == N_GROUPS - 1),
                     )
-                nc.tensor.matmul_mx(
-                    out=q_sums[(b, half)][:],
-                    lhsT=cq_words[:, g, b * N : (b + 1) * N].bitcast(FP8X4),
-                    lhsT_scale=cq_scales[:, g, b * N : (b + 1) * N],
-                    rhs=words[:].bitcast(FP8X4),
-                    rhs_scale=scales[:],
-                    start=(g == 0),
-                    stop=(g == N_GROUPS - 1),
-                )
 
         table = const.tile([P, 2, PAIRS, 2], F32)
 
@@ -280,17 +287,17 @@ def tile_multilatentattention_pa_k_kernel(tc, x, Wqa, Wqb, out):
         for step in range(2 * N_GROUPS + 1):
             run(load_wqa, step + 1)
             run(load_wqb, step - N_GROUPS + 1)
-            run(round_cq, step - 2)
+            run(turn_wqa, step + 1)
+            run(turn_wqb, step - N_GROUPS + 1)
             run(regroup_wqa, step)
             if step == 0:
                 quantise(x_words[:], x_scales[:], x_grouped[:])
             if step == 1:
                 nc.scalar.activation(out=table[:], in_=part[:], func=ACT.Sin, scale=2.0 * math.pi)
-            run(turn_wqb, step - N_GROUPS + 1)
+            run(round_cq, step - 2)
             run(regroup_wqb, step - N_GROUPS)
             run(quantise_wqa, step - 1)
             run(first_product, step - 1)
-            run(turn_wqa, step + 1)
             run(quantise_cq, step - 3)
             run(second_product, step - N_GROUPS - 1)
 

@@ -28,10 +28,13 @@ HEADS_PER_HALF = BANK // QH
 PAIRS = ROPE // 2
 
 RUN = 8
-WQA_TENSOR_FOURS = 32
-WQA_SCALAR_FOURS = (0, 0, 0, 12)
-WQB_TENSOR_COLUMNS = 128
-WQB_SCALAR_COLUMNS = (144, 320, 416)
+IDENTITY_COLUMNS = 128
+SECOND_IDENTITY = (0, 1, 4, 7, 10, 13)
+WQA_TENSOR_EIGHTS = IDENTITY_COLUMNS // (2 * PACK)
+WQA_SCALAR_EIGHTS = 6
+WQB_SCALAR_COLUMNS = {1: 416, 2: 336}
+WQB_SCALAR_FIRST = (80, 256)
+WQB_SCALAR_LAST = 320
 RAW_BUFS = 8
 
 ROUND_MAGIC = 1.5 * 2.0**23
@@ -155,7 +158,7 @@ def tile_multilatentattention_pa_k_kernel(tc, x, Wqa, Wqb, out):
 
         def turn_wqa(g):
             wqa_turned[g] = q_psum.tile(
-                [P, PACK, WQA_TENSOR_FOURS, PACK],
+                [P, PACK, IDENTITY_COLUMNS // PACK, PACK],
                 BF16,
                 name="wqa_turned_%d" % (g % 4),
                 tag="q_bank_%d" % (g % 4),
@@ -163,7 +166,7 @@ def tile_multilatentattention_pa_k_kernel(tc, x, Wqa, Wqb, out):
             nc.tensor.matmul(
                 out=wqa_turned[g][:].rearrange("p t m j -> p j m t"),
                 lhsT=identity_bf16[:],
-                rhs=wqa_rows[g][:, :, 0 : PACK * WQA_TENSOR_FOURS].rearrange("p j (m t) -> p j m t", t=PACK),
+                rhs=wqa_rows[g][:, :, 0:IDENTITY_COLUMNS].rearrange("p j (m t) -> p j m t", t=PACK),
                 start=True,
                 stop=True,
             )
@@ -173,14 +176,14 @@ def tile_multilatentattention_pa_k_kernel(tc, x, Wqa, Wqb, out):
                 [P, K_PASS, PACK], BF16, name="wqa_grouped", tag="wqa_grouped", align_bytes=64
             )
             by_place = wqa_grouped[g][:].rearrange("p (t m) j -> p t m j", t=PACK)
-            placed = wqa_grouped[g][:].rearrange("p (t m) j -> p m j t", t=PACK)
-            columns = wqa_rows[g][:].rearrange("p j (m t) -> p m j t", t=PACK)
-            first = WQA_TENSOR_FOURS
-            second = first + WQA_SCALAR_FOURS[min(g, len(WQA_SCALAR_FOURS) - 1)]
-            nc.scalar.copy(out=by_place[:, :, 0:first, :], in_=wqa_turned[g][:])
+            placed = wqa_grouped[g][:].rearrange("p (t m n) j -> p m j n t", t=PACK, n=2)
+            columns = wqa_rows[g][:].rearrange("p j (m n t) -> p m j n t", t=PACK, n=2)
+            first = WQA_TENSOR_EIGHTS
+            second = first + (0 if g < 3 else WQA_SCALAR_EIGHTS)
+            nc.scalar.copy(out=by_place[:, :, 0 : 2 * first, :], in_=wqa_turned[g][:])
             if second > first:
                 nc.scalar.copy(out=placed[:, first:second], in_=columns[:, first:second])
-            nc.vector.tensor_copy(out=placed[:, second:P], in_=columns[:, second:P])
+            nc.vector.tensor_copy(out=placed[:, second:], in_=columns[:, second:])
 
         def quantise_wqa(g):
             wqa_words[g] = work.tile([P, K_PASS], U32, name="wqa_words", tag="wqa_words", align_bytes=64)
@@ -227,26 +230,35 @@ def tile_multilatentattention_pa_k_kernel(tc, x, Wqa, Wqb, out):
                 in_=Wqb[g * K_PASS : (g + 1) * K_PASS, :].rearrange("(p t) w -> p t w", t=PACK),
             )
 
+        def identity_columns(g):
+            return IDENTITY_COLUMNS * (2 if g in SECOND_IDENTITY else 1)
+
         def turn_wqb(g):
-            shape = [P, WQB_TENSOR_COLUMNS, PACK]
+            shape = [P, identity_columns(g), PACK]
             if g < 2:
                 wqb_turned[g] = q_psum.tile(shape, BF16, name="wqb_turned_%d" % g, tag="q_bank_%d" % g)
             else:
                 wqb_turned[g] = cq_psum.tile(shape, BF16, name="wqb_turned", tag="cq_bank")
-            nc.tensor.matmul(
-                out=wqb_turned[g][:].rearrange("p w t -> p t w"),
-                lhsT=identity_bf16[:],
-                rhs=wqb_rows[g][:, :, 0:WQB_TENSOR_COLUMNS],
-                start=True,
-                stop=True,
-            )
+            for c in range(0, identity_columns(g), IDENTITY_COLUMNS):
+                cols = slice(c, c + IDENTITY_COLUMNS)
+                nc.tensor.matmul(
+                    out=wqb_turned[g][:, cols, :].rearrange("p w t -> p t w"),
+                    lhsT=identity_bf16[:],
+                    rhs=wqb_rows[g][:, :, cols],
+                    start=True,
+                    stop=True,
+                )
 
         def regroup_wqb(g):
             wqb_grouped[g] = work.tile(
                 [P, HQ, PACK], BF16, name="wqb_grouped", tag="wqb_grouped", align_bytes=64
             )
-            first = WQB_TENSOR_COLUMNS
-            second = first + WQB_SCALAR_COLUMNS[min(g, len(WQB_SCALAR_COLUMNS) - 1)]
+            first = identity_columns(g)
+            second = first + WQB_SCALAR_COLUMNS[first // IDENTITY_COLUMNS]
+            if g < len(WQB_SCALAR_FIRST):
+                second = first + WQB_SCALAR_FIRST[g]
+            if g == N_GROUPS - 1:
+                second = first + WQB_SCALAR_LAST
             nc.scalar.copy(out=wqb_grouped[g][:, 0:first, :], in_=wqb_turned[g][:])
             regroup(nc.scalar.copy, wqb_grouped[g][:, first:second, :], wqb_rows[g][:, :, first:second])
             regroup(nc.vector.tensor_copy, wqb_grouped[g][:, second:HQ, :], wqb_rows[g][:, :, second:HQ])
@@ -322,22 +334,33 @@ def tile_multilatentattention_pa_k_kernel(tc, x, Wqa, Wqb, out):
             )
 
         middle = HEADS_PER_HALF // 2
-        parts = ((0, middle), (middle, HEADS_PER_HALF))
-        pieces = []
-        for half in range(HALVES):
-            for b in range(B):
-                q = q_sums[(b, half)][:].rearrange("p (h d) -> p h d", d=QH)
-                result = results.tile([P, HEADS_PER_HALF, QH], F32)
-                terms = results.tile([P, 2, HEADS_PER_HALF, ROPE], F32)
-                nc.scalar.copy(out=result[:, :, 0:NOPE], in_=q[:, :, 0:NOPE])
-                last = (half, b) == (HALVES - 1, B - 1)
-                for h0, h1 in parts if last else ((0, HEADS_PER_HALF),):
-                    multiply(q, terms, h0, h1)
-                    if half == 0:
-                        add(nc.gpsimd, result, terms, h0, h1)
-                        store(b, half, h0, h1, result)
-                    else:
-                        pieces.append((b, half, h0, h1, result, terms))
-        for b, half, h0, h1, result, terms in pieces:
-            add(nc.vector, result, terms, h0, h1)
-            store(b, half, h0, h1, result)
+        banks = [(half, b) for half in range(HALVES) for b in range(B)]
+        q, result, terms = {}, {}, {}
+        for bank in banks:
+            half, b = bank
+            q[bank] = q_sums[(b, half)][:].rearrange("p (h d) -> p h d", d=QH)
+            result[bank] = results.tile([P, HEADS_PER_HALF, QH], F32, name="result", tag="result")
+            terms[bank] = results.tile([P, 2, HEADS_PER_HALF, ROPE], F32, name="terms", tag="terms")
+
+        def copy_unrotated(bank):
+            nc.scalar.copy(out=result[bank][:, :, 0:NOPE], in_=q[bank][:, :, 0:NOPE])
+
+        def finish(engine, bank, h0, h1):
+            half, b = bank
+            add(engine, result[bank], terms[bank], h0, h1)
+            store(b, half, h0, h1, result[bank])
+
+        multiply(q[banks[0]], terms[banks[0]], 0, HEADS_PER_HALF)
+        copy_unrotated(banks[1])
+        copy_unrotated(banks[0])
+        finish(nc.gpsimd, banks[0], 0, HEADS_PER_HALF)
+        multiply(q[banks[1]], terms[banks[1]], 0, HEADS_PER_HALF)
+        finish(nc.gpsimd, banks[1], 0, HEADS_PER_HALF)
+        copy_unrotated(banks[2])
+        multiply(q[banks[2]], terms[banks[2]], 0, HEADS_PER_HALF)
+        copy_unrotated(banks[3])
+        multiply(q[banks[3]], terms[banks[3]], 0, middle)
+        multiply(q[banks[3]], terms[banks[3]], middle, HEADS_PER_HALF)
+        finish(nc.vector, banks[2], 0, HEADS_PER_HALF)
+        finish(nc.vector, banks[3], 0, middle)
+        finish(nc.vector, banks[3], middle, HEADS_PER_HALF)

@@ -55,8 +55,8 @@ def tile_multilatentattention_pa_k_kernel(tc, x, Wqa, Wqb, out):
 
         def regroup(copy, grouped, rows):
             copy(
-                out=grouped.rearrange("p (c i) t -> p c t i", i=RUN),
-                in_=rows.rearrange("p t (c i) -> p c t i", i=RUN),
+                out=grouped.rearrange("p (c i) (u e) -> p c u i e", i=RUN, e=2),
+                in_=rows.rearrange("p (u e) (c i) -> p c u i e", i=RUN, e=2),
             )
 
         def quantise(words, scales, grouped):

import math
from contextlib import ExitStack

import concourse.mybir as mybir
from concourse.masks import make_identity

F32 = mybir.dt.float32
BF16 = mybir.dt.bfloat16
U32 = mybir.dt.uint32
U8 = mybir.dt.uint8
FP8X4 = mybir.dt.float8_e4m3fn_x4
ALU = mybir.AluOpType
ACT = mybir.ActivationFunctionType

B, N, E, H, NOPE, ROPE, QR = 2, 128, 512, 16, 32, 32, 8192
QH = NOPE + ROPE
HQ = H * QH
BASE = 10000.0

P = 128
PACK = 4
K_PASS = P * PACK
BANK = 512

N_GROUPS = QR // K_PASS
HALVES = HQ // BANK
HEADS_PER_HALF = BANK // QH
PAIRS = ROPE // 2

RUN = 8
IDENTITY_COLUMNS = 128
SECOND_IDENTITY = (0, 1, 4, 7, 10, 13)
WQA_TENSOR_EIGHTS = IDENTITY_COLUMNS // (2 * PACK)
WQA_SCALAR_EIGHTS = 6
WQB_SCALAR_COLUMNS = {1: 416, 2: 336}
WQB_SCALAR_FIRST = (80, 256)
WQB_SCALAR_LAST = 320
RAW_BUFS = 8

ROUND_MAGIC = 1.5 * 2.0**23

FLOPS = 2 * B * N * E * QR + 2 * B * N * QR * HQ


def tile_multilatentattention_pa_k_kernel(tc, x, Wqa, Wqb, out):
    nc = tc.nc
    with ExitStack() as ctx:
        ctx.enter_context(tc.manual_schedule())
        const = ctx.enter_context(tc.tile_pool(name="const", bufs=1))
        raw = ctx.enter_context(tc.tile_pool(name="raw", bufs=RAW_BUFS))
        work = ctx.enter_context(tc.tile_pool(name="work", bufs=3))
        results = ctx.enter_context(tc.tile_pool(name="results", bufs=B * HALVES))
        cq_psum = ctx.enter_context(tc.psum_pool(name="cq_psum", bufs=4))
        q_psum = ctx.enter_context(tc.psum_pool(name="q_psum", bufs=1))

        def regroup(copy, grouped, rows):
            copy(
                out=grouped.rearrange("p (c i) (u e) -> p c u i e", i=RUN, e=2),
                in_=rows.rearrange("p (u e) (c i) -> p c u i e", i=RUN, e=2),
            )

        def quantise(words, scales, grouped):
            nc.vector.quantize_mx(
                out=words.bitcast(FP8X4),
                scales=scales,
                in_=grouped.rearrange("p w t -> p (w t)"),
            )

        x_rows = const.tile([P, B, E], BF16)
        nc.sync.dma_start(out=x_rows[:], in_=x.rearrange("b n e -> n b e"))

        position = const.tile([P, 1], F32)
        nc.gpsimd.iota(
            position[:],
            pattern=[[0, 1]],
            base=0,
            channel_multiplier=1,
            allow_small_or_imprecise_dtypes=True,
        )
        identity = const.tile([P, P], F32)
        make_identity(nc, identity[:])

        turns = const.tile([P, PAIRS], F32)
        ratio = BASE ** (-2.0 / ROPE)
        filled = 4
        for i in range(filled):
            nc.vector.tensor_scalar(
                out=turns[:, i : i + 1],
                in0=position[:],
                scalar1=ratio**i / (2.0 * math.pi),
                scalar2=None,
                op0=ALU.mult,
            )
        while filled < PAIRS:
            nc.vector.tensor_scalar(
                out=turns[:, filled : 2 * filled],
                in0=turns[:, 0:filled],
                scalar1=ratio**filled,
                scalar2=None,
                op0=ALU.mult,
            )
            filled *= 2
        phase = const.tile([P, 2, PAIRS, 2], F32)
        nc.vector.tensor_scalar(
            out=phase[:, 0],
            in0=turns[:].unsqueeze(2).to_broadcast([P, PAIRS, 2]),
            scalar1=0.25,
            scalar2=None,
            op0=ALU.add,
        )
        nc.vector.tensor_copy(out=phase[:, 1, :, 0], in_=turns[:])
        nc.vector.tensor_scalar(
            out=phase[:, 1, :, 1], in0=turns[:], scalar1=-1.0, scalar2=None, op0=ALU.mult
        )
        whole = const.tile([P, 2, PAIRS, 2], F32)
        nc.vector.tensor_scalar(
            out=whole[:],
            in0=phase[:],
            scalar1=ROUND_MAGIC,
            scalar2=ROUND_MAGIC,
            op0=ALU.add,
            op1=ALU.subtract,
        )
        part = const.tile([P, 2, PAIRS, 2], F32)
        nc.vector.tensor_tensor(out=part[:], in0=phase[:], in1=whole[:], op=ALU.subtract)

        identity_bf16 = const.tile([P, P], BF16)
        nc.vector.tensor_copy(out=identity_bf16[:], in_=identity[:])

        x_pairs = x_rows[:].bitcast(F32).rearrange("n b (p u) -> n b u p", u=2)
        x_turned = cq_psum.tile([P, PACK, P], F32, name="x_turned", tag="cq_bank")
        for b in range(B):
            for u in range(2):
                nc.tensor.transpose(x_turned[:, 2 * b + u, :], x_pairs[:, b, u, :], identity[:])
        x_grouped = const.tile([P, B * N, PACK], BF16, align_bytes=64)
        nc.scalar.copy(
            out=x_grouped[:].bitcast(F32).rearrange("p (b n) u -> p b n u", b=B),
            in_=x_turned[:].rearrange("p (b u) n -> p b n u", u=2),
        )
        x_words = const.tile([P, B * N], U32, align_bytes=64)
        x_scales = const.tile([P, B * N], U8, align_bytes=64)

        cq_words = const.tile([P, N_GROUPS, B * N], U32, align_bytes=64)
        cq_scales = const.tile([P, N_GROUPS, B * N], U8, align_bytes=64)
        q_sums = {}
        wqa_rows, wqa_turned = {}, {}
        wqa_grouped, wqa_words, wqa_scales = {}, {}, {}
        cq_banks, cq_grouped = {}, {}
        wqb_rows, wqb_turned = {}, {}
        wqb_grouped = {}

        def load_wqa(g):
            wqa_rows[g] = raw.tile([P, PACK, K_PASS], BF16, name="wqa_rows", tag="wqa_rows")
            nc.sync.dma_start(
                out=wqa_rows[g][:],
                in_=Wqa[:, g * K_PASS : (g + 1) * K_PASS].rearrange("(p t) w -> p t w", t=PACK),
            )

        def turn_wqa(g):
            wqa_turned[g] = q_psum.tile(
                [P, PACK, IDENTITY_COLUMNS // PACK, PACK],
                BF16,
                name="wqa_turned_%d" % (g % 4),
                tag="q_bank_%d" % (g % 4),
            )
            nc.tensor.matmul(
                out=wqa_turned[g][:].rearrange("p t m j -> p j m t"),
                lhsT=identity_bf16[:],
                rhs=wqa_rows[g][:, :, 0:IDENTITY_COLUMNS].rearrange("p j (m t) -> p j m t", t=PACK),
                start=True,
                stop=True,
            )

        def regroup_wqa(g):
            wqa_grouped[g] = work.tile(
                [P, K_PASS, PACK], BF16, name="wqa_grouped", tag="wqa_grouped", align_bytes=64
            )
            by_place = wqa_grouped[g][:].rearrange("p (t m) j -> p t m j", t=PACK)
            placed = wqa_grouped[g][:].rearrange("p (t m n) j -> p m j n t", t=PACK, n=2)
            columns = wqa_rows[g][:].rearrange("p j (m n t) -> p m j n t", t=PACK, n=2)
            first = WQA_TENSOR_EIGHTS
            second = first + (0 if g < 3 else WQA_SCALAR_EIGHTS)
            nc.scalar.copy(out=by_place[:, :, 0 : 2 * first, :], in_=wqa_turned[g][:])
            if second > first:
                nc.scalar.copy(out=placed[:, first:second], in_=columns[:, first:second])
            nc.vector.tensor_copy(out=placed[:, second:], in_=columns[:, second:])

        def quantise_wqa(g):
            wqa_words[g] = work.tile([P, K_PASS], U32, name="wqa_words", tag="wqa_words", align_bytes=64)
            wqa_scales[g] = work.tile([P, K_PASS], U8, name="wqa_scales", tag="wqa_scales", align_bytes=64)
            quantise(wqa_words[g][:], wqa_scales[g][:], wqa_grouped[g][:])

        def first_product(g):
            for b in range(B):
                cq_banks[(g, b)] = cq_psum.tile([P, PACK, N], F32, name="cq_bank", tag="cq_bank")
                for t in range(PACK):
                    nc.tensor.matmul_mx(
                        out=cq_banks[(g, b)][:, t, :],
                        lhsT=wqa_words[g][:, t * P : (t + 1) * P].bitcast(FP8X4),
                        lhsT_scale=wqa_scales[g][:, t * P : (t + 1) * P],
                        rhs=x_words[:, b * N : (b + 1) * N].bitcast(FP8X4),
                        rhs_scale=x_scales[:, b * N : (b + 1) * N],
                        start=True,
                        stop=True,
                    )

        def round_cq(g):
            if g % 2 == 0:
                cq_grouped[g // 2] = work.tile(
                    [P, 2, B * N, PACK], BF16, name="cq_grouped", tag="cq_grouped", align_bytes=64
                )
            for b in range(B):
                nc.scalar.copy(
                    out=cq_grouped[g // 2][:, g % 2, b * N : (b + 1) * N, :],
                    in_=cq_banks[(g, b)][:].rearrange("p t n -> p n t"),
                )

        def quantise_cq(g):
            if g % 2 == 1:
                quantise(
                    cq_words[:, g - 1 : g + 1, :].rearrange("p g n -> p (g n)"),
                    cq_scales[:, g - 1 : g + 1, :].rearrange("p g n -> p (g n)"),
                    cq_grouped[g // 2][:].rearrange("p g n t -> p (g n) t"),
                )

        def load_wqb(g):
            wqb_rows[g] = raw.tile([P, PACK, HQ], BF16, name="wqb_rows", tag="wqb_rows")
            nc.sync.dma_start(
                out=wqb_rows[g][:],
                in_=Wqb[g * K_PASS : (g + 1) * K_PASS, :].rearrange("(p t) w -> p t w", t=PACK),
            )

        def identity_columns(g):
            return IDENTITY_COLUMNS * (2 if g in SECOND_IDENTITY else 1)

        def turn_wqb(g):
            shape = [P, identity_columns(g), PACK]
            if g < 2:
                wqb_turned[g] = q_psum.tile(shape, BF16, name="wqb_turned_%d" % g, tag="q_bank_%d" % g)
            else:
                wqb_turned[g] = cq_psum.tile(shape, BF16, name="wqb_turned", tag="cq_bank")
            for c in range(0, identity_columns(g), IDENTITY_COLUMNS):
                cols = slice(c, c + IDENTITY_COLUMNS)
                nc.tensor.matmul(
                    out=wqb_turned[g][:, cols, :].rearrange("p w t -> p t w"),
                    lhsT=identity_bf16[:],
                    rhs=wqb_rows[g][:, :, cols],
                    start=True,
                    stop=True,
                )

        def regroup_wqb(g):
            wqb_grouped[g] = work.tile(
                [P, HQ, PACK], BF16, name="wqb_grouped", tag="wqb_grouped", align_bytes=64
            )
            first = identity_columns(g)
            second = first + WQB_SCALAR_COLUMNS[first // IDENTITY_COLUMNS]
            if g < len(WQB_SCALAR_FIRST):
                second = first + WQB_SCALAR_FIRST[g]
            if g == N_GROUPS - 1:
                second = first + WQB_SCALAR_LAST
            nc.scalar.copy(out=wqb_grouped[g][:, 0:first, :], in_=wqb_turned[g][:])
            regroup(nc.scalar.copy, wqb_grouped[g][:, first:second, :], wqb_rows[g][:, :, first:second])
            regroup(nc.vector.tensor_copy, wqb_grouped[g][:, second:HQ, :], wqb_rows[g][:, :, second:HQ])

        def second_product(g):
            words = work.tile([P, HQ], U32, name="wqb_words", tag="wqb_words", align_bytes=64)
            scales = work.tile([P, HQ], U8, name="wqb_scales", tag="wqb_scales", align_bytes=64)
            width = HQ if g < N_GROUPS - 1 else BANK
            for c in range(0, HQ, width):
                cols = slice(c, c + width)
                quantise(words[:, cols], scales[:, cols], wqb_grouped[g][:, cols, :])
            for half in range(HALVES):
                cols = slice(half * BANK, (half + 1) * BANK)
                for b in range(B):
                    if g == 0:
                        bank = HALVES * b + half
                        q_sums[(b, half)] = q_psum.tile(
                            [P, BANK], F32, name="q_sums_%d" % bank, tag="q_bank_%d" % bank
                        )
                    nc.tensor.matmul_mx(
                        out=q_sums[(b, half)][:],
                        lhsT=cq_words[:, g, b * N : (b + 1) * N].bitcast(FP8X4),
                        lhsT_scale=cq_scales[:, g, b * N : (b + 1) * N],
                        rhs=words[:, cols].bitcast(FP8X4),
                        rhs_scale=scales[:, cols],
                        start=(g == 0),
                        stop=(g == N_GROUPS - 1),
                    )

        table = const.tile([P, 2, PAIRS, 2], F32)

        def run(stage, g):
            if 0 <= g < N_GROUPS:
                stage(g)

        load_wqa(0)
        turn_wqa(0)
        for step in range(2 * N_GROUPS + 1):
            run(load_wqa, step + 1)
            run(load_wqb, step - N_GROUPS + 1)
            run(turn_wqa, step + 1)
            run(turn_wqb, step - N_GROUPS + 1)
            run(regroup_wqa, step)
            if step == 0:
                quantise(x_words[:], x_scales[:], x_grouped[:])
            if step == 1:
                nc.scalar.activation(out=table[:], in_=part[:], func=ACT.Sin, scale=2.0 * math.pi)
            run(round_cq, step - 2)
            run(regroup_wqb, step - N_GROUPS)
            run(quantise_wqa, step - 1)
            run(first_product, step - 1)
            run(quantise_cq, step - 3)
            run(second_product, step - N_GROUPS - 1)

        def store(b, half, h0, h1, result):
            heads = slice(half * HEADS_PER_HALF + h0, half * HEADS_PER_HALF + h1)
            nc.sync.dma_start(out=out[b, heads].rearrange("h n d -> n h d"), in_=result[:, h0:h1])

        def multiply(q, terms, h0, h1):
            wide = [P, 2, h1 - h0, ROPE]
            nc.vector.tensor_mul(
                out=terms[:, :, h0:h1],
                in0=q[:, h0:h1, NOPE:QH].unsqueeze(1).to_broadcast(wide),
                in1=table[:].rearrange("p r i e -> p r (i e)").unsqueeze(2).to_broadcast(wide),
            )

        def add(engine, result, terms, h0, h1):
            engine.tensor_tensor(
                out=result[:, h0:h1, NOPE:QH].rearrange("p h (i e) -> p h i e", e=2),
                in0=terms[:, 0, h0:h1].rearrange("p h (i e) -> p h i e", e=2),
                in1=terms[:, 1, h0:h1].rearrange("p h (i e) -> p h i e", e=2)[:, :, :, ::-1],
                op=ALU.add,
            )

        middle = HEADS_PER_HALF // 2
        banks = [(half, b) for half in range(HALVES) for b in range(B)]
        q, result, terms = {}, {}, {}
        for bank in banks:
            half, b = bank
            q[bank] = q_sums[(b, half)][:].rearrange("p (h d) -> p h d", d=QH)
            result[bank] = results.tile([P, HEADS_PER_HALF, QH], F32, name="result", tag="result")
            terms[bank] = results.tile([P, 2, HEADS_PER_HALF, ROPE], F32, name="terms", tag="terms")

        def copy_unrotated(bank):
            nc.scalar.copy(out=result[bank][:, :, 0:NOPE], in_=q[bank][:, :, 0:NOPE])

        def finish(engine, bank, h0, h1):
            half, b = bank
            add(engine, result[bank], terms[bank], h0, h1)
            store(b, half, h0, h1, result[bank])

        multiply(q[banks[0]], terms[banks[0]], 0, HEADS_PER_HALF)
        copy_unrotated(banks[1])
        copy_unrotated(banks[0])
        finish(nc.gpsimd, banks[0], 0, HEADS_PER_HALF)
        multiply(q[banks[1]], terms[banks[1]], 0, HEADS_PER_HALF)
        finish(nc.gpsimd, banks[1], 0, HEADS_PER_HALF)
        copy_unrotated(banks[2])
        multiply(q[banks[2]], terms[banks[2]], 0, HEADS_PER_HALF)
        copy_unrotated(banks[3])
        multiply(q[banks[3]], terms[banks[3]], 0, middle)
        multiply(q[banks[3]], terms[banks[3]], middle, HEADS_PER_HALF)
        finish(nc.vector, banks[2], 0, HEADS_PER_HALF)
        finish(nc.vector, banks[3], 0, middle)
        finish(nc.vector, banks[3], middle, HEADS_PER_HALF)
